import numpy as np
import ml_dtypes


def mxq(x, axis, fmt="e4m3"):
    dtype, down = {"e4m3": (ml_dtypes.float8_e4m3fn, 7), "e5m2": (ml_dtypes.float8_e5m2, 14)}[fmt]
    v = np.moveaxis(np.asarray(x, np.float32).astype(ml_dtypes.bfloat16).astype(np.float64), axis, -1)
    blocks = v.reshape(v.shape[:-1] + (-1, 32))
    amax = np.abs(blocks).max(-1, keepdims=True)
    byte = np.maximum(np.where(amax > 0, np.frexp(amax)[1] - 1 + 127, 0) - down, 1)
    scale = np.exp2(byte - 127.0)
    codes = (blocks / scale).astype(np.float32).astype(dtype).astype(np.float64)
    return np.moveaxis((codes * scale).reshape(v.shape), -1, axis)


WIDE = False


def mx_kscale(k):
    if not WIDE:
        return np.ones(k)
    levels = np.array([10, -10, 5, -5, 0])
    a = np.random.permutation(np.resize(levels, k // 512 * 4)).reshape(k // 512, 4)
    idx = np.arange(k)
    return np.exp2(a[idx // 512, idx % 128 // 32])


BF16 = ml_dtypes.bfloat16


def bf(x):
    return np.asarray(x, np.float32).astype(BF16)


def f64(x):
    return np.asarray(x).astype(np.float64)


E2M1 = np.array([0.0, 0.5, 1.0, 1.5, 2.0, 3.0, 4.0, 6.0, -0.0, -0.5, -1.0, -1.5, -2.0, -3.0, -4.0, -6.0])


def pack_weight(w, fmt):
    k, n = w.shape
    w = f64(bf(w)).reshape(k // 32, 32, n)
    amax = np.abs(w).max(1)
    if fmt == "e4m3":
        byte = np.frexp(amax)[1] - 1 + 127 - 7
    else:
        mant, ex = np.frexp(amax / 6.0)
        byte = np.where(mant > 0.5, ex, ex - 1) + 127
    byte = np.clip(np.where(amax > 0, byte, 1), 1, 254)
    scaled = (w * np.exp2(127.0 - byte)[:, None, :]).reshape(k, n).astype(np.float32)
    by_word = np.ascontiguousarray(scaled.reshape(k // 512, 128, 4, n).transpose(0, 1, 3, 2))
    if fmt == "e4m3":
        words = by_word.astype(ml_dtypes.float8_e4m3fn).view(np.uint8)
    else:
        c = by_word.astype(ml_dtypes.float4_e2m1fn).view(np.uint8) & 0xF
        words = c[..., 0::2] | (c[..., 1::2] << 4)
    return np.ascontiguousarray(words), np.ascontiguousarray(byte.astype(np.uint8).reshape(k // 512, 16, n))


def unpack_weight(words, scales, fmt):
    g, p, n, _ = words.shape
    if fmt == "e4m3":
        vals = np.ascontiguousarray(words).view(ml_dtypes.float8_e4m3fn).astype(np.float64)
    else:
        nib = np.empty((g, p, n, 4), np.uint8)
        nib[..., 0::2] = words & 0xF
        nib[..., 1::2] = words >> 4
        vals = E2M1[nib]
    vals = vals * np.repeat(np.exp2(scales.astype(np.float64) - 127.0), 8, axis=1)[..., None]
    return vals.transpose(0, 1, 3, 2).reshape(g * 512, n)


B, CIN, COUT, T, R, C = 2, 16384, 128, 8, 4, 4


def setup_inputs():
    s = mx_kscale(CIN)
    x = np.random.standard_normal((B, CIN, T, R, C)) * s[None, :, None, None, None]
    W = np.random.standard_normal((7 * COUT, CIN)) * 0.5 / np.sqrt(CIN) / s[None, :]
    words, scales = pack_weight(np.ascontiguousarray(W.T), "e4m3")
    return {"x": bf(x), "W_words": words, "W_scales": scales}


def _shift(a, axis, d):
    pads = [(0, 0)] * a.ndim
    idx = [slice(None)] * a.ndim
    if d > 0:
        pads[axis] = (1, 0)
        idx[axis] = slice(0, -1)
    else:
        pads[axis] = (0, 1)
        idx[axis] = slice(1, None)
    return np.pad(a, pads)[tuple(idx)]


def reference(x, W_words, W_scales):
    cout = W_words.shape[2] // 7
    xq = mxq(f64(x), 1, "e4m3")
    Wq = unpack_weight(W_words, W_scales, "e4m3").T
    all_out = xq.transpose(0, 2, 3, 4, 1) @ Wq.T
    a = all_out.reshape(*all_out.shape[:4], 7, cout)
    out = a[..., 0, :]
    out = out + _shift(a[..., 1, :], 1, +1)
    out = out + _shift(a[..., 2, :], 1, -1)
    out = out + _shift(a[..., 3, :], 2, +1)
    out = out + _shift(a[..., 4, :], 2, -1)
    out = out + _shift(a[..., 5, :], 3, +1)
    out = out + _shift(a[..., 6, :], 3, -1)
    return np.transpose(out, (0, 4, 1, 2, 3))

@@ -1,0 +1,157 @@
+from contextlib import ExitStack
+
+import concourse.mybir as mybir
+
+BF16 = mybir.dt.bfloat16
+F32 = mybir.dt.float32
+I32 = mybir.dt.int32
+U8 = mybir.dt.uint8
+U32 = mybir.dt.uint32
+FP8X4 = mybir.dt.float8_e4m3fn_x4
+
+P = 128
+PACK = 4
+K_PASS = P * PACK
+
+BATCH, CIN, COUT = 2, 16384, 128
+T, R, C = 8, 4, 4
+VOXELS = T * R * C
+COLS = BATCH * VOXELS
+DIRECTIONS = 7
+W_COLS = DIRECTIONS * COUT
+PASSES = CIN // K_PASS
+
+CHUNK = 4
+CHUNKS = PASSES // CHUNK
+QUADRANTS = 4
+ROWS_PER_QUADRANT = 4
+
+SHIFTS = (
+    (VOXELS, R * C),
+    (VOXELS, -R * C),
+    (R * C, C),
+    (R * C, -C),
+    (C, 1),
+    (C, -1),
+)
+
+FLOPS = 2 * COLS * CIN * W_COLS
+
+
+def add_shifted(nc, total, term, period, step):
+    dst = total.rearrange("p (n i) -> p n i", i=period)
+    src = term.rearrange("p (n i) -> p n i", i=period)
+    if step > 0:
+        dst, src = dst[:, :, step:period], src[:, :, 0 : period - step]
+    else:
+        dst, src = dst[:, :, 0 : period + step], src[:, :, -step:period]
+    nc.vector.tensor_tensor(out=dst, in0=dst, in1=src, op=mybir.AluOpType.add)
+
+
+def tile_stackeddirectionalconv3d_k_kernel(tc, x, W_words, W_scales, out):
+    nc = tc.nc
+
+    x_runs = x.rearrange("b (g p j) t r c -> b p g (j t r c)", p=P, j=PACK)
+    w_word_rows = W_words.rearrange("g p n j -> g p (n j)").bitcast(I32)
+    w_scale_rows = W_scales.bitcast(I32)
+    out_rows = out.rearrange("b o t r c -> o b (t r c)")
+
+    with ExitStack() as ctx:
+        ctx.enter_context(tc.manual_schedule())
+        keep = ctx.enter_context(tc.tile_pool(name="keep", bufs=1))
+        w_pool = ctx.enter_context(tc.tile_pool(name="w", bufs=CHUNKS))
+        raw_pool = ctx.enter_context(tc.tile_pool(name="raw", bufs=4))
+        grouped_pool = ctx.enter_context(tc.tile_pool(name="grouped", bufs=3))
+        xq_pool = ctx.enter_context(tc.tile_pool(name="xq", bufs=3))
+        psum = ctx.enter_context(tc.psum_pool(name="psum", bufs=1))
+
+        w_planes = keep.tile([P, CHUNKS, W_COLS], U8, align_bytes=64)
+        nc.vector.memset(w_planes[:].rearrange("p c n -> p (c n)").bitcast(I32), 0)
+
+        x_raw = {}
+        x_grouped = {}
+        x_codes = {}
+        x_planes = {}
+        w_words = {}
+
+        def load_x(c):
+            x_raw[c] = raw_pool.tile([P, CHUNK, BATCH, PACK * VOXELS], BF16, name="x_raw")
+            for b in range(BATCH):
+                nc.sync.dma_start(
+                    out=x_raw[c][:, :, b, :], in_=x_runs[b, :, c * CHUNK : (c + 1) * CHUNK, :]
+                )
+
+        def load_w_scales(c):
+            for quadrant in range(QUADRANTS):
+                first = quadrant * ROWS_PER_QUADRANT
+                nc.sync.dma_start(
+                    out=w_planes[32 * quadrant : 32 * quadrant + 16, c, :].bitcast(I32),
+                    in_=w_scale_rows[
+                        c * CHUNK : (c + 1) * CHUNK, first : first + ROWS_PER_QUADRANT, :
+                    ],
+                )
+
+        def load_w_words(c):
+            w_words[c] = w_pool.tile([P, CHUNK, W_COLS], U32, name="w_words", align_bytes=64)
+            for j in range(CHUNK):
+                nc.sync.dma_start(
+                    out=w_words[c][:, j, :].bitcast(I32), in_=w_word_rows[c * CHUNK + j]
+                )
+
+        def group_x(c):
+            x_grouped[c] = grouped_pool.tile(
+                [P, CHUNK * BATCH, VOXELS, PACK], BF16, name="x_grouped", align_bytes=64
+            )
+            nc.vector.tensor_copy(
+                out=x_grouped[c][:],
+                in_=x_raw[c][:].rearrange("p g b (j v) -> p (g b) v j", j=PACK),
+            )
+
+        def quantise_x(c):
+            x_codes[c] = xq_pool.tile([P, CHUNK, COLS], U32, name="x_codes", align_bytes=64)
+            x_planes[c] = xq_pool.tile([P, CHUNK, COLS], U8, name="x_planes", align_bytes=64)
+            nc.vector.quantize_mx(
+                out=x_codes[c][:].rearrange("p g w -> p (g w)").bitcast(FP8X4),
+                scales=x_planes[c][:].rearrange("p g w -> p (g w)"),
+                in_=x_grouped[c][:].rearrange("p n v j -> p (n v j)"),
+            )
+
+        y = [psum.tile([P, COLS], F32, name="y%d" % d) for d in range(DIRECTIONS)]
+
+        def multiply(c):
+            for j in range(CHUNK):
+                g = c * CHUNK + j
+                for d in range(DIRECTIONS):
+                    channels = slice(d * COUT, (d + 1) * COUT)
+                    nc.tensor.matmul_mx(
+                        out=y[d][:],
+                        lhsT=w_words[c][:, j, channels].bitcast(FP8X4),
+                        lhsT_scale=w_planes[4 * j : P, c, channels],
+                        rhs=x_codes[c][:, j, :].bitcast(FP8X4),
+                        rhs_scale=x_planes[c][:, j, :],
+                        start=(g == 0),
+                        stop=(g == PASSES - 1),
+                    )
+
+        load_x(0)
+        for c in range(CHUNKS):
+            load_w_scales(c)
+        load_x(1)
+        for c in range(CHUNKS):
+            load_w_words(c)
+            if c + 2 < CHUNKS:
+                load_x(c + 2)
+
+        group_x(0)
+        for c in range(CHUNKS):
+            if c + 1 < CHUNKS:
+                group_x(c + 1)
+            quantise_x(c)
+            multiply(c)
+
+        total = keep.tile([P, COLS], F32)
+        nc.vector.tensor_copy(out=total[:], in_=y[0][:])
+        for d in range(1, DIRECTIONS):
+            period, step = SHIFTS[d - 1]
+            add_shifted(nc, total[:], y[d][:], period, step)
+        nc.sync.dma_start(out=out_rows, in_=total[:].rearrange("p (b v) -> p b v", b=BATCH))

@@ -134,11 +134,12 @@ def tile_stackeddirectionalconv3d_k_kernel(tc, x, W_words, W_scales, out):
                     )
 
         load_x(0)
-        for c in range(CHUNKS):
-            load_w_scales(c)
+        load_w_scales(0)
         load_x(1)
         for c in range(CHUNKS):
             load_w_words(c)
+            if c + 1 < CHUNKS:
+                load_w_scales(c + 1)
             if c + 2 < CHUNKS:
                 load_x(c + 2)
 

@@ -23,6 +23,7 @@ PASSES = CIN // K_PASS
 
 CHUNK = 4
 CHUNKS = PASSES // CHUNK
+X_LEAD = 2
 QUADRANTS = 4
 ROWS_PER_QUADRANT = 4
 
@@ -38,14 +39,12 @@ SHIFTS = (
 FLOPS = 2 * COLS * CIN * W_COLS
 
 
-def add_shifted(nc, total, term, period, step):
+def shifted_views(total, term, period, step):
     dst = total.rearrange("p (n i) -> p n i", i=period)
     src = term.rearrange("p (n i) -> p n i", i=period)
     if step > 0:
-        dst, src = dst[:, :, step:period], src[:, :, 0 : period - step]
-    else:
-        dst, src = dst[:, :, 0 : period + step], src[:, :, -step:period]
-    nc.vector.tensor_tensor(out=dst, in0=dst, in1=src, op=mybir.AluOpType.add)
+        return dst[:, :, step:period], src[:, :, 0 : period - step]
+    return dst[:, :, 0 : period + step], src[:, :, -step:period]
 
 
 def tile_stackeddirectionalconv3d_k_kernel(tc, x, W_words, W_scales, out):
@@ -62,11 +61,14 @@ def tile_stackeddirectionalconv3d_k_kernel(tc, x, W_words, W_scales, out):
         w_pool = ctx.enter_context(tc.tile_pool(name="w", bufs=CHUNKS))
         raw_pool = ctx.enter_context(tc.tile_pool(name="raw", bufs=4))
         grouped_pool = ctx.enter_context(tc.tile_pool(name="grouped", bufs=3))
-        xq_pool = ctx.enter_context(tc.tile_pool(name="xq", bufs=3))
+        xq_pool = ctx.enter_context(tc.tile_pool(name="xq", bufs=4))
         psum = ctx.enter_context(tc.psum_pool(name="psum", bufs=1))
 
         w_planes = keep.tile([P, CHUNKS, W_COLS], U8, align_bytes=64)
         nc.vector.memset(w_planes[:].rearrange("p c n -> p (c n)").bitcast(I32), 0)
+
+        sums = [keep.tile([P, COLS], F32, name="sum%d" % i) for i in range(2)]
+        nc.vector.memset(sums[1][:], 0.0)
 
         x_raw = {}
         x_grouped = {}
@@ -133,15 +135,15 @@ def tile_stackeddirectionalconv3d_k_kernel(tc, x, W_words, W_scales, out):
                         stop=(g == PASSES - 1),
                     )
 
-        load_x(0)
+        for c in range(X_LEAD):
+            load_x(c)
         load_w_scales(0)
-        load_x(1)
         for c in range(CHUNKS):
+            if c + X_LEAD < CHUNKS:
+                load_x(c + X_LEAD)
             load_w_words(c)
             if c + 1 < CHUNKS:
                 load_w_scales(c + 1)
-            if c + 2 < CHUNKS:
-                load_x(c + 2)
 
         group_x(0)
         for c in range(CHUNKS):
@@ -150,9 +152,15 @@ def tile_stackeddirectionalconv3d_k_kernel(tc, x, W_words, W_scales, out):
             quantise_x(c)
             multiply(c)
 
-        total = keep.tile([P, COLS], F32)
-        nc.vector.tensor_copy(out=total[:], in_=y[0][:])
+        nc.scalar.copy(out=sums[0][:], in_=y[0][:])
         for d in range(1, DIRECTIONS):
             period, step = SHIFTS[d - 1]
-            add_shifted(nc, total[:], y[d][:], period, step)
-        nc.sync.dma_start(out=out_rows, in_=total[:].rearrange("p (b v) -> p b v", b=BATCH))
+            dst, src = shifted_views(sums[d % 2][:], y[d][:], period, step)
+            if d == 1:
+                nc.scalar.copy(out=dst, in_=src)
+            else:
+                nc.vector.tensor_tensor(out=dst, in0=dst, in1=src, op=mybir.AluOpType.add)
+        nc.vector.tensor_tensor(
+            out=sums[0][:], in0=sums[0][:], in1=sums[1][:], op=mybir.AluOpType.add
+        )
+        nc.sync.dma_start(out=out_rows, in_=sums[0][:].rearrange("p (b v) -> p b v", b=BATCH))

@@ -52,7 +52,7 @@ def tile_stackeddirectionalconv3d_k_kernel(tc, x, W_words, W_scales, out):
 
     x_runs = x.rearrange("b (g p j) t r c -> b p g (j t r c)", p=P, j=PACK)
     w_word_rows = W_words.rearrange("g p n j -> g p (n j)").bitcast(I32)
-    w_scale_rows = W_scales.bitcast(I32)
+    w_scale_rows = W_scales.bitcast(F32)
     out_rows = out.rearrange("b o t r c -> o b (t r c)")
 
     with ExitStack() as ctx:
@@ -86,8 +86,8 @@ def tile_stackeddirectionalconv3d_k_kernel(tc, x, W_words, W_scales, out):
         def load_w_scales(c):
             for quadrant in range(QUADRANTS):
                 first = quadrant * ROWS_PER_QUADRANT
-                nc.sync.dma_start(
-                    out=w_planes[32 * quadrant : 32 * quadrant + 16, c, :].bitcast(I32),
+                nc.gpsimd.dma_start(
+                    out=w_planes[32 * quadrant : 32 * quadrant + 16, c, :].bitcast(F32),
                     in_=w_scale_rows[
                         c * CHUNK : (c + 1) * CHUNK, first : first + ROWS_PER_QUADRANT, :
                     ],
@@ -137,13 +137,12 @@ def tile_stackeddirectionalconv3d_k_kernel(tc, x, W_words, W_scales, out):
 
         for c in range(X_LEAD):
             load_x(c)
-        load_w_scales(0)
+        for c in range(CHUNKS):
+            load_w_scales(c)
         for c in range(CHUNKS):
             if c + X_LEAD < CHUNKS:
                 load_x(c + X_LEAD)
             load_w_words(c)
-            if c + 1 < CHUNKS:
-                load_w_scales(c + 1)
 
         group_x(0)
         for c in range(CHUNKS):

@@ -84,9 +84,10 @@ def tile_stackeddirectionalconv3d_k_kernel(tc, x, W_words, W_scales, out):
                 )
 
         def load_w_scales(c):
+            queue = nc.sync if c < CHUNKS // 2 else nc.gpsimd
             for quadrant in range(QUADRANTS):
                 first = quadrant * ROWS_PER_QUADRANT
-                nc.gpsimd.dma_start(
+                queue.dma_start(
                     out=w_planes[32 * quadrant : 32 * quadrant + 16, c, :].bitcast(F32),
                     in_=w_scale_rows[
                         c * CHUNK : (c + 1) * CHUNK, first : first + ROWS_PER_QUADRANT, :
@@ -137,12 +138,13 @@ def tile_stackeddirectionalconv3d_k_kernel(tc, x, W_words, W_scales, out):
 
         for c in range(X_LEAD):
             load_x(c)
-        for c in range(CHUNKS):
-            load_w_scales(c)
+        load_w_scales(0)
         for c in range(CHUNKS):
             if c + X_LEAD < CHUNKS:
                 load_x(c + X_LEAD)
             load_w_words(c)
+            if c + 1 < CHUNKS:
+                load_w_scales(c + 1)
 
         group_x(0)
         for c in range(CHUNKS):

@@ -23,6 +23,7 @@ PASSES = CIN // K_PASS
 
 CHUNK = 4
 CHUNKS = PASSES // CHUNK
+LAST = CHUNKS - 1
 X_LEAD = 2
 QUADRANTS = 4
 ROWS_PER_QUADRANT = 4
@@ -69,6 +70,10 @@ def tile_stackeddirectionalconv3d_k_kernel(tc, x, W_words, W_scales, out):
 
         sums = [keep.tile([P, COLS], F32, name="sum%d" % i) for i in range(2)]
         nc.vector.memset(sums[1][:], 0.0)
+        result = keep.tile([P, COLS], F32, name="result")
+
+        moved_codes = keep.tile([P, DIRECTIONS - 1, CHUNK, COLS], U32, name="moved_codes", align_bytes=64)
+        moved_planes = keep.tile([P, DIRECTIONS - 1, CHUNK, COLS], U8, name="moved_planes", align_bytes=64)
 
         x_raw = {}
         x_grouped = {}
@@ -79,7 +84,7 @@ def tile_stackeddirectionalconv3d_k_kernel(tc, x, W_words, W_scales, out):
         def load_x(c):
             x_raw[c] = raw_pool.tile([P, CHUNK, BATCH, PACK * VOXELS], BF16, name="x_raw")
             for b in range(BATCH):
-                nc.sync.dma_start(
+                nc.scalar.dma_start(
                     out=x_raw[c][:, :, b, :], in_=x_runs[b, :, c * CHUNK : (c + 1) * CHUNK, :]
                 )
 
@@ -113,27 +118,51 @@ def tile_stackeddirectionalconv3d_k_kernel(tc, x, W_words, W_scales, out):
         def quantise_x(c):
             x_codes[c] = xq_pool.tile([P, CHUNK, COLS], U32, name="x_codes", align_bytes=64)
             x_planes[c] = xq_pool.tile([P, CHUNK, COLS], U8, name="x_planes", align_bytes=64)
+            if c == LAST:
+                nc.vector.memset(x_planes[c][:].rearrange("p g w -> p (g w)").bitcast(I32), 0)
             nc.vector.quantize_mx(
                 out=x_codes[c][:].rearrange("p g w -> p (g w)").bitcast(FP8X4),
                 scales=x_planes[c][:].rearrange("p g w -> p (g w)"),
                 in_=x_grouped[c][:].rearrange("p n v j -> p (n v j)"),
             )
 
+        def shift_x():
+            codes = x_codes[LAST][:].rearrange("p g w -> p (g w)").bitcast(I32)
+            plane_bytes = x_planes[LAST][:].rearrange("p g w -> p (g w)")
+            for d in range(1, DIRECTIONS):
+                period, step = SHIFTS[d - 1]
+                dst, src = shifted_views(
+                    moved_codes[:, d - 1, :, :].rearrange("p g w -> p (g w)").bitcast(I32),
+                    codes,
+                    period,
+                    step,
+                )
+                nc.vector.tensor_copy(out=dst, in_=src)
+                moved_bytes = moved_planes[:, d - 1, :, :].rearrange("p g w -> p (g w)")
+                if step % 4 == 0:
+                    dst, src = shifted_views(
+                        moved_bytes.bitcast(I32), plane_bytes.bitcast(I32), period // 4, step // 4
+                    )
+                else:
+                    dst, src = shifted_views(moved_bytes, plane_bytes, period, step)
+                nc.vector.tensor_copy(out=dst, in_=src)
+
         y = [psum.tile([P, COLS], F32, name="y%d" % d) for d in range(DIRECTIONS)]
+        tail = psum.tile([P, COLS], F32, name="tail")
 
         def multiply(c):
             for j in range(CHUNK):
-                g = c * CHUNK + j
                 for d in range(DIRECTIONS):
                     channels = slice(d * COUT, (d + 1) * COUT)
+                    moved = c == LAST and d > 0
                     nc.tensor.matmul_mx(
-                        out=y[d][:],
+                        out=tail[:] if c == LAST else y[d][:],
                         lhsT=w_words[c][:, j, channels].bitcast(FP8X4),
                         lhsT_scale=w_planes[4 * j : P, c, channels],
-                        rhs=x_codes[c][:, j, :].bitcast(FP8X4),
-                        rhs_scale=x_planes[c][:, j, :],
-                        start=(g == 0),
-                        stop=(g == PASSES - 1),
+                        rhs=(moved_codes[:, d - 1, j, :] if moved else x_codes[c][:, j, :]).bitcast(FP8X4),
+                        rhs_scale=moved_planes[:, d - 1, j, :] if moved else x_planes[c][:, j, :],
+                        start=(j == 0 and (c == 0 or (c == LAST and d == 0))),
+                        stop=(j == CHUNK - 1 and (c == LAST - 1 or (c == LAST and d == DIRECTIONS - 1))),
                     )
 
         for c in range(X_LEAD):
@@ -147,10 +176,15 @@ def tile_stackeddirectionalconv3d_k_kernel(tc, x, W_words, W_scales, out):
                 load_w_scales(c + 1)
 
         group_x(0)
-        for c in range(CHUNKS):
-            if c + 1 < CHUNKS:
-                group_x(c + 1)
+        for c in range(LAST):
+            group_x(c + 1)
             quantise_x(c)
+            if c == 1:
+                nc.vector.memset(moved_codes[:].rearrange("p d g w -> p (d g w)").bitcast(I32), 0)
+                nc.vector.memset(moved_planes[:].rearrange("p d g w -> p (d g w)").bitcast(I32), 0)
+            if c == LAST - 1:
+                quantise_x(LAST)
+                shift_x()
             multiply(c)
 
         nc.scalar.copy(out=sums[0][:], in_=y[0][:])
@@ -164,4 +198,6 @@ def tile_stackeddirectionalconv3d_k_kernel(tc, x, W_words, W_scales, out):
         nc.vector.tensor_tensor(
             out=sums[0][:], in0=sums[0][:], in1=sums[1][:], op=mybir.AluOpType.add
         )
-        nc.sync.dma_start(out=out_rows, in_=sums[0][:].rearrange("p (b v) -> p b v", b=BATCH))
+        multiply(LAST)
+        nc.vector.tensor_tensor(out=result[:], in0=tail[:], in1=sums[0][:], op=mybir.AluOpType.add)
+        nc.sync.dma_start(out=out_rows, in_=result[:].rearrange("p (b v) -> p b v", b=BATCH))

@@ -24,6 +24,8 @@ PASSES = CIN // K_PASS
 CHUNK = 4
 CHUNKS = PASSES // CHUNK
 LAST = CHUNKS - 1
+TAIL_PASSES = 2
+FIRST_TAIL = PASSES - TAIL_PASSES
 X_LEAD = 2
 QUADRANTS = 4
 ROWS_PER_QUADRANT = 4
@@ -69,11 +71,18 @@ def tile_stackeddirectionalconv3d_k_kernel(tc, x, W_words, W_scales, out):
         nc.vector.memset(w_planes[:].rearrange("p c n -> p (c n)").bitcast(I32), 0)
 
         sums = [keep.tile([P, COLS], F32, name="sum%d" % i) for i in range(2)]
+        nc.vector.memset(sums[0][:], 0.0)
         nc.vector.memset(sums[1][:], 0.0)
         result = keep.tile([P, COLS], F32, name="result")
 
-        moved_codes = keep.tile([P, DIRECTIONS - 1, CHUNK, COLS], U32, name="moved_codes", align_bytes=64)
-        moved_planes = keep.tile([P, DIRECTIONS - 1, CHUNK, COLS], U8, name="moved_planes", align_bytes=64)
+        moved_codes = keep.tile(
+            [P, DIRECTIONS - 1, TAIL_PASSES, COLS], U32, name="moved_codes", align_bytes=64
+        )
+        moved_planes = keep.tile(
+            [P, DIRECTIONS - 1, TAIL_PASSES, COLS], U8, name="moved_planes", align_bytes=64
+        )
+        nc.vector.memset(moved_codes[:].rearrange("p d g w -> p (d g w)").bitcast(I32), 0)
+        nc.vector.memset(moved_planes[:].rearrange("p d g w -> p (d g w)").bitcast(I32), 0)
 
         x_raw = {}
         x_grouped = {}
@@ -127,8 +136,9 @@ def tile_stackeddirectionalconv3d_k_kernel(tc, x, W_words, W_scales, out):
             )
 
         def shift_x():
-            codes = x_codes[LAST][:].rearrange("p g w -> p (g w)").bitcast(I32)
-            plane_bytes = x_planes[LAST][:].rearrange("p g w -> p (g w)")
+            first = CHUNK - TAIL_PASSES
+            codes = x_codes[LAST][:, first:CHUNK, :].rearrange("p g w -> p (g w)").bitcast(I32)
+            plane_bytes = x_planes[LAST][:, first:CHUNK, :].rearrange("p g w -> p (g w)")
             for d in range(1, DIRECTIONS):
                 period, step = SHIFTS[d - 1]
                 dst, src = shifted_views(
@@ -147,23 +157,34 @@ def tile_stackeddirectionalconv3d_k_kernel(tc, x, W_words, W_scales, out):
                     dst, src = shifted_views(moved_bytes, plane_bytes, period, step)
                 nc.vector.tensor_copy(out=dst, in_=src)
 
-        y = [psum.tile([P, COLS], F32, name="y%d" % d) for d in range(DIRECTIONS)]
+        y = [None] + [psum.tile([P, COLS], F32, name="y%d" % d) for d in range(1, DIRECTIONS)]
         tail = psum.tile([P, COLS], F32, name="tail")
 
-        def multiply(c):
-            for j in range(CHUNK):
-                for d in range(DIRECTIONS):
-                    channels = slice(d * COUT, (d + 1) * COUT)
-                    moved = c == LAST and d > 0
-                    nc.tensor.matmul_mx(
-                        out=tail[:] if c == LAST else y[d][:],
-                        lhsT=w_words[c][:, j, channels].bitcast(FP8X4),
-                        lhsT_scale=w_planes[4 * j : P, c, channels],
-                        rhs=(moved_codes[:, d - 1, j, :] if moved else x_codes[c][:, j, :]).bitcast(FP8X4),
-                        rhs_scale=moved_planes[:, d - 1, j, :] if moved else x_planes[c][:, j, :],
-                        start=(j == 0 and (c == 0 or (c == LAST and d == 0))),
-                        stop=(j == CHUNK - 1 and (c == LAST - 1 or (c == LAST and d == DIRECTIONS - 1))),
-                    )
+        def multiply(g):
+            c, j = divmod(g, CHUNK)
+            in_tail = g >= FIRST_TAIL
+            for d in range(DIRECTIONS):
+                channels = slice(d * COUT, (d + 1) * COUT)
+                moved = in_tail and d > 0
+                if d == 0 or in_tail:
+                    group = tail
+                    start = g == 0
+                    stop = g == PASSES - 1 and d == DIRECTIONS - 1
+                else:
+                    group = y[d]
+                    start = g == 0
+                    stop = g == FIRST_TAIL - 1
+                nc.tensor.matmul_mx(
+                    out=group[:],
+                    lhsT=w_words[c][:, j, channels].bitcast(FP8X4),
+                    lhsT_scale=w_planes[4 * j : P, c, channels],
+                    rhs=(
+                        moved_codes[:, d - 1, g - FIRST_TAIL, :] if moved else x_codes[c][:, j, :]
+                    ).bitcast(FP8X4),
+                    rhs_scale=moved_planes[:, d - 1, g - FIRST_TAIL, :] if moved else x_planes[c][:, j, :],
+                    start=start,
+                    stop=stop,
+                )
 
         for c in range(X_LEAD):
             load_x(c)
@@ -179,25 +200,25 @@ def tile_stackeddirectionalconv3d_k_kernel(tc, x, W_words, W_scales, out):
         for c in range(LAST):
             group_x(c + 1)
             quantise_x(c)
-            if c == 1:
-                nc.vector.memset(moved_codes[:].rearrange("p d g w -> p (d g w)").bitcast(I32), 0)
-                nc.vector.memset(moved_planes[:].rearrange("p d g w -> p (d g w)").bitcast(I32), 0)
             if c == LAST - 1:
                 quantise_x(LAST)
                 shift_x()
-            multiply(c)
+            for g in range(c * CHUNK, (c + 1) * CHUNK):
+                multiply(g)
+        for g in range(LAST * CHUNK, FIRST_TAIL):
+            multiply(g)
 
-        nc.scalar.copy(out=sums[0][:], in_=y[0][:])
         for d in range(1, DIRECTIONS):
             period, step = SHIFTS[d - 1]
             dst, src = shifted_views(sums[d % 2][:], y[d][:], period, step)
-            if d == 1:
+            if d <= 2:
                 nc.scalar.copy(out=dst, in_=src)
             else:
                 nc.vector.tensor_tensor(out=dst, in0=dst, in1=src, op=mybir.AluOpType.add)
         nc.vector.tensor_tensor(
             out=sums[0][:], in0=sums[0][:], in1=sums[1][:], op=mybir.AluOpType.add
         )
-        multiply(LAST)
+        for g in range(FIRST_TAIL, PASSES):
+            multiply(g)
         nc.vector.tensor_tensor(out=result[:], in0=tail[:], in1=sums[0][:], op=mybir.AluOpType.add)
         nc.sync.dma_start(out=out_rows, in_=result[:].rearrange("p (b v) -> p b v", b=BATCH))

@@ -24,6 +24,7 @@ PASSES = CIN // K_PASS
 CHUNK = 4
 CHUNKS = PASSES // CHUNK
 LAST = CHUNKS - 1
+HALF = CHUNK // 2
 TAIL_PASSES = 2
 FIRST_TAIL = PASSES - TAIL_PASSES
 X_LEAD = 2
@@ -115,24 +116,30 @@ def tile_stackeddirectionalconv3d_k_kernel(tc, x, W_words, W_scales, out):
                     out=w_words[c][:, j, :].bitcast(I32), in_=w_word_rows[c * CHUNK + j]
                 )
 
-        def group_x(c):
+        def new_x_tiles(c):
             x_grouped[c] = grouped_pool.tile(
-                [P, CHUNK * BATCH, VOXELS, PACK], BF16, name="x_grouped", align_bytes=64
+                [P, CHUNK, BATCH * VOXELS * PACK], BF16, name="x_grouped", align_bytes=64
             )
-            nc.vector.tensor_copy(
-                out=x_grouped[c][:],
-                in_=x_raw[c][:].rearrange("p g b (j v) -> p (g b) v j", j=PACK),
-            )
-
-        def quantise_x(c):
             x_codes[c] = xq_pool.tile([P, CHUNK, COLS], U32, name="x_codes", align_bytes=64)
             x_planes[c] = xq_pool.tile([P, CHUNK, COLS], U8, name="x_planes", align_bytes=64)
             if c == LAST:
                 nc.vector.memset(x_planes[c][:].rearrange("p g w -> p (g w)").bitcast(I32), 0)
+
+        def group_x(c, half):
+            passes = slice(half * HALF, (half + 1) * HALF)
+            nc.vector.tensor_copy(
+                out=x_grouped[c][:, passes, :].rearrange(
+                    "p g (b v j) -> p (g b) v j", b=BATCH, j=PACK
+                ),
+                in_=x_raw[c][:, passes, :, :].rearrange("p g b (j v) -> p (g b) v j", j=PACK),
+            )
+
+        def quantise_x(c, half):
+            passes = slice(half * HALF, (half + 1) * HALF)
             nc.vector.quantize_mx(
-                out=x_codes[c][:].rearrange("p g w -> p (g w)").bitcast(FP8X4),
-                scales=x_planes[c][:].rearrange("p g w -> p (g w)"),
-                in_=x_grouped[c][:].rearrange("p n v j -> p (n v j)"),
+                out=x_codes[c][:, passes, :].rearrange("p g w -> p (g w)").bitcast(FP8X4),
+                scales=x_planes[c][:, passes, :].rearrange("p g w -> p (g w)"),
+                in_=x_grouped[c][:, passes, :].rearrange("p g n -> p (g n)"),
             )
 
         def shift_x():
@@ -196,17 +203,17 @@ def tile_stackeddirectionalconv3d_k_kernel(tc, x, W_words, W_scales, out):
             if c + 1 < CHUNKS:
                 load_w_scales(c + 1)
 
-        group_x(0)
-        for c in range(LAST):
-            group_x(c + 1)
-            quantise_x(c)
-            if c == LAST - 1:
-                quantise_x(LAST)
+        for c in range(CHUNKS):
+            new_x_tiles(c)
+            halves = (1, 0) if c == LAST else (0, 1)
+            for half in halves:
+                group_x(c, half)
+            for half in halves:
+                quantise_x(c, half)
+            if c == LAST:
                 shift_x()
-            for g in range(c * CHUNK, (c + 1) * CHUNK):
+            for g in range(c * CHUNK, min((c + 1) * CHUNK, FIRST_TAIL)):
                 multiply(g)
-        for g in range(LAST * CHUNK, FIRST_TAIL):
-            multiply(g)
 
         for d in range(1, DIRECTIONS):
             period, step = SHIFTS[d - 1]

from contextlib import ExitStack

import concourse.mybir as mybir

BF16 = mybir.dt.bfloat16
F32 = mybir.dt.float32
I32 = mybir.dt.int32
U8 = mybir.dt.uint8
U32 = mybir.dt.uint32
FP8X4 = mybir.dt.float8_e4m3fn_x4

P = 128
PACK = 4
K_PASS = P * PACK

BATCH, CIN, COUT = 2, 16384, 128
T, R, C = 8, 4, 4
VOXELS = T * R * C
COLS = BATCH * VOXELS
DIRECTIONS = 7
W_COLS = DIRECTIONS * COUT
PASSES = CIN // K_PASS

CHUNK = 4
CHUNKS = PASSES // CHUNK
LAST = CHUNKS - 1
HALF = CHUNK // 2
TAIL_PASSES = 2
FIRST_TAIL = PASSES - TAIL_PASSES
X_LEAD = 2
QUADRANTS = 4
ROWS_PER_QUADRANT = 4

SHIFTS = (
    (VOXELS, R * C),
    (VOXELS, -R * C),
    (R * C, C),
    (R * C, -C),
    (C, 1),
    (C, -1),
)

FLOPS = 2 * COLS * CIN * W_COLS


def shifted_views(total, term, period, step):
    dst = total.rearrange("p (n i) -> p n i", i=period)
    src = term.rearrange("p (n i) -> p n i", i=period)
    if step > 0:
        return dst[:, :, step:period], src[:, :, 0 : period - step]
    return dst[:, :, 0 : period + step], src[:, :, -step:period]


def tile_stackeddirectionalconv3d_k_kernel(tc, x, W_words, W_scales, out):
    nc = tc.nc

    x_runs = x.rearrange("b (g p j) t r c -> b p g (j t r c)", p=P, j=PACK)
    w_word_rows = W_words.rearrange("g p n j -> g p (n j)").bitcast(I32)
    w_scale_rows = W_scales.bitcast(F32)
    out_rows = out.rearrange("b o t r c -> o b (t r c)")

    with ExitStack() as ctx:
        ctx.enter_context(tc.manual_schedule())
        keep = ctx.enter_context(tc.tile_pool(name="keep", bufs=1))
        w_pool = ctx.enter_context(tc.tile_pool(name="w", bufs=CHUNKS))
        raw_pool = ctx.enter_context(tc.tile_pool(name="raw", bufs=4))
        grouped_pool = ctx.enter_context(tc.tile_pool(name="grouped", bufs=3))
        xq_pool = ctx.enter_context(tc.tile_pool(name="xq", bufs=4))
        psum = ctx.enter_context(tc.psum_pool(name="psum", bufs=1))

        w_planes = keep.tile([P, CHUNKS, W_COLS], U8, align_bytes=64)
        nc.vector.memset(w_planes[:].rearrange("p c n -> p (c n)").bitcast(I32), 0)

        sums = [keep.tile([P, COLS], F32, name="sum%d" % i) for i in range(2)]
        nc.vector.memset(sums[0][:], 0.0)
        nc.vector.memset(sums[1][:], 0.0)
        result = keep.tile([P, COLS], F32, name="result")

        moved_codes = keep.tile(
            [P, DIRECTIONS - 1, TAIL_PASSES, COLS], U32, name="moved_codes", align_bytes=64
        )
        moved_planes = keep.tile(
            [P, DIRECTIONS - 1, TAIL_PASSES, COLS], U8, name="moved_planes", align_bytes=64
        )
        nc.vector.memset(moved_codes[:].rearrange("p d g w -> p (d g w)").bitcast(I32), 0)
        nc.vector.memset(moved_planes[:].rearrange("p d g w -> p (d g w)").bitcast(I32), 0)

        x_raw = {}
        x_grouped = {}
        x_codes = {}
        x_planes = {}
        w_words = {}

        def load_x(c):
            x_raw[c] = raw_pool.tile([P, CHUNK, BATCH, PACK * VOXELS], BF16, name="x_raw")
            for b in range(BATCH):
                nc.scalar.dma_start(
                    out=x_raw[c][:, :, b, :], in_=x_runs[b, :, c * CHUNK : (c + 1) * CHUNK, :]
                )

        def load_w_scales(c):
            queue = nc.sync if c < CHUNKS // 2 else nc.gpsimd
            for quadrant in range(QUADRANTS):
                first = quadrant * ROWS_PER_QUADRANT
                queue.dma_start(
                    out=w_planes[32 * quadrant : 32 * quadrant + 16, c, :].bitcast(F32),
                    in_=w_scale_rows[
                        c * CHUNK : (c + 1) * CHUNK, first : first + ROWS_PER_QUADRANT, :
                    ],
                )

        def load_w_words(c):
            w_words[c] = w_pool.tile([P, CHUNK, W_COLS], U32, name="w_words", align_bytes=64)
            for j in range(CHUNK):
                nc.sync.dma_start(
                    out=w_words[c][:, j, :].bitcast(I32), in_=w_word_rows[c * CHUNK + j]
                )

        def new_x_tiles(c):
            x_grouped[c] = grouped_pool.tile(
                [P, CHUNK, BATCH * VOXELS * PACK], BF16, name="x_grouped", align_bytes=64
            )
            x_codes[c] = xq_pool.tile([P, CHUNK, COLS], U32, name="x_codes", align_bytes=64)
            x_planes[c] = xq_pool.tile([P, CHUNK, COLS], U8, name="x_planes", align_bytes=64)
            if c == LAST:
                nc.vector.memset(x_planes[c][:].rearrange("p g w -> p (g w)").bitcast(I32), 0)

        def group_x(c, half):
            passes = slice(half * HALF, (half + 1) * HALF)
            nc.vector.tensor_copy(
                out=x_grouped[c][:, passes, :].rearrange(
                    "p g (b v j) -> p (g b) v j", b=BATCH, j=PACK
                ),
                in_=x_raw[c][:, passes, :, :].rearrange("p g b (j v) -> p (g b) v j", j=PACK),
            )

        def quantise_x(c, half):
            passes = slice(half * HALF, (half + 1) * HALF)
            nc.vector.quantize_mx(
                out=x_codes[c][:, passes, :].rearrange("p g w -> p (g w)").bitcast(FP8X4),
                scales=x_planes[c][:, passes, :].rearrange("p g w -> p (g w)"),
                in_=x_grouped[c][:, passes, :].rearrange("p g n -> p (g n)"),
            )

        def shift_x():
            first = CHUNK - TAIL_PASSES
            codes = x_codes[LAST][:, first:CHUNK, :].rearrange("p g w -> p (g w)").bitcast(I32)
            plane_bytes = x_planes[LAST][:, first:CHUNK, :].rearrange("p g w -> p (g w)")
            for d in range(1, DIRECTIONS):
                period, step = SHIFTS[d - 1]
                dst, src = shifted_views(
                    moved_codes[:, d - 1, :, :].rearrange("p g w -> p (g w)").bitcast(I32),
                    codes,
                    period,
                    step,
                )
                nc.vector.tensor_copy(out=dst, in_=src)
                moved_bytes = moved_planes[:, d - 1, :, :].rearrange("p g w -> p (g w)")
                if step % 4 == 0:
                    dst, src = shifted_views(
                        moved_bytes.bitcast(I32), plane_bytes.bitcast(I32), period // 4, step // 4
                    )
                else:
                    dst, src = shifted_views(moved_bytes, plane_bytes, period, step)
                nc.vector.tensor_copy(out=dst, in_=src)

        y = [None] + [psum.tile([P, COLS], F32, name="y%d" % d) for d in range(1, DIRECTIONS)]
        tail = psum.tile([P, COLS], F32, name="tail")

        def multiply(g):
            c, j = divmod(g, CHUNK)
            in_tail = g >= FIRST_TAIL
            for d in range(DIRECTIONS):
                channels = slice(d * COUT, (d + 1) * COUT)
                moved = in_tail and d > 0
                if d == 0 or in_tail:
                    group = tail
                    start = g == 0
                    stop = g == PASSES - 1 and d == DIRECTIONS - 1
                else:
                    group = y[d]
                    start = g == 0
                    stop = g == FIRST_TAIL - 1
                nc.tensor.matmul_mx(
                    out=group[:],
                    lhsT=w_words[c][:, j, channels].bitcast(FP8X4),
                    lhsT_scale=w_planes[4 * j : P, c, channels],
                    rhs=(
                        moved_codes[:, d - 1, g - FIRST_TAIL, :] if moved else x_codes[c][:, j, :]
                    ).bitcast(FP8X4),
                    rhs_scale=moved_planes[:, d - 1, g - FIRST_TAIL, :] if moved else x_planes[c][:, j, :],
                    start=start,
                    stop=stop,
                )

        for c in range(X_LEAD):
            load_x(c)
        load_w_scales(0)
        for c in range(CHUNKS):
            if c + X_LEAD < CHUNKS:
                load_x(c + X_LEAD)
            load_w_words(c)
            if c + 1 < CHUNKS:
                load_w_scales(c + 1)

        for c in range(CHUNKS):
            new_x_tiles(c)
            halves = (1, 0) if c == LAST else (0, 1)
            for half in halves:
                group_x(c, half)
            for half in halves:
                quantise_x(c, half)
            if c == LAST:
                shift_x()
            for g in range(c * CHUNK, min((c + 1) * CHUNK, FIRST_TAIL)):
                multiply(g)

        for d in range(1, DIRECTIONS):
            period, step = SHIFTS[d - 1]
            dst, src = shifted_views(sums[d % 2][:], y[d][:], period, step)
            if d <= 2:
                nc.scalar.copy(out=dst, in_=src)
            else:
                nc.vector.tensor_tensor(out=dst, in0=dst, in1=src, op=mybir.AluOpType.add)
        nc.vector.tensor_tensor(
            out=sums[0][:], in0=sums[0][:], in1=sums[1][:], op=mybir.AluOpType.add
        )
        for g in range(FIRST_TAIL, PASSES):
            multiply(g)
        nc.vector.tensor_tensor(out=result[:], in0=tail[:], in1=sums[0][:], op=mybir.AluOpType.add)
        nc.sync.dma_start(out=out_rows, in_=result[:].rearrange("p (b v) -> p b v", b=BATCH))
